import numpy as np
import ml_dtypes

BF16 = ml_dtypes.bfloat16


def bf(x):
    return np.asarray(x, np.float32).astype(BF16)


def f32(x):
    return np.asarray(x, np.float32)


def f64(x):
    return np.asarray(x).astype(np.float64)


def striped(idx):
    return np.tile(idx.reshape(-1, 16).T, (8, 1))


S, D, M, N, R = 1024, 128, 256, 512, 3
INV_SQRT_MUL = 1.0 / np.sqrt(D)
INV_SQRT_R = 1.0 / np.sqrt(R)


def setup_inputs():
    return {"table": bf(np.random.standard_normal((S, D))), "w": bf(np.random.standard_normal((D, M))), "k1": f32(np.random.standard_normal((D, N))), "k00": f32(np.random.standard_normal((D, N))), "k11": f32(np.random.standard_normal((D, N))), "hv": f32(np.random.standard_normal((D, R, N))), "wprod": bf(np.random.standard_normal((D, D))), "wout": bf(np.random.standard_normal((D, D))), "offs": striped(np.random.permutation(S)[:N])}


def reference(table, w, k1, k00, k11, hv, wprod, wout, offs):
    idx = offs[:16].T.reshape(-1)
    x = f64(table)[idx].T
    h = (f64(w)[:, :D].T @ x) * INV_SQRT_MUL
    sc = (f64(w)[:, D:].T @ x) * INV_SQRT_MUL
    q = np.sum(f64(hv) * f64(hv), axis=1) * INV_SQRT_R
    a = f64(k1) * h + f64(k00) * h * h + f64(k11) * q
    p = (f64(wprod).T @ a) * INV_SQRT_MUL
    return (f64(wout).T @ p) * INV_SQRT_MUL + sc

@@ -1,0 +1,83 @@
+import math
+
+import concourse.mybir as mybir
+from concourse.masks import make_identity
+
+P = 128
+S = 1024
+N = 512
+R = 3
+BLOCKS = S // P
+
+FLOPS = 4 * 2 * P * P * N
+
+BF16 = mybir.dt.bfloat16
+F32 = mybir.dt.float32
+U16 = mybir.dt.uint16
+MULT = mybir.AluOpType.mult
+ADD = mybir.AluOpType.add
+COPY = mybir.ActivationFunctionType.Copy
+SQUARE = mybir.ActivationFunctionType.Square
+
+INV_SQRT_P = 1.0 / math.sqrt(P)
+QUARTER_ROOT = 3.0 ** -0.25
+
+
+def tile_corrproductblock_kernel(tc, table, w, k1, k00, k11, hv, wprod, wout, offs, out):
+    nc = tc.nc
+    with tc.tile_pool(name="held", bufs=1) as held, tc.psum_pool(name="psum", bufs=1) as psum:
+        offsets = held.tile([P, N // 16], U16, name="offsets")
+        nc.sync.dma_start(offsets[:], offs)
+        rows = held.tile([P, BLOCKS, P], BF16, name="rows")
+        nc.sync.dma_start(rows[:], table.rearrange("(b p) d -> p b d", p=P))
+        w_sb = held.tile([P, 2 * P], BF16, name="w_sb")
+        nc.sync.dma_start(w_sb[:], w)
+        hv_sb = held.tile([P, R, N], F32, name="hv_sb")
+        nc.scalar.dma_start(hv_sb[:], hv)
+        k11_sb = held.tile([P, N], F32, name="k11_sb")
+        nc.sync.dma_start(k11_sb[:], k11)
+        k00_sb = held.tile([P, N], F32, name="k00_sb")
+        nc.sync.dma_start(k00_sb[:], k00)
+        k1_sb = held.tile([P, N], F32, name="k1_sb")
+        nc.sync.dma_start(k1_sb[:], k1)
+        wprod_sb = held.tile([P, P], BF16, name="wprod_sb")
+        nc.scalar.dma_start(wprod_sb[:], wprod)
+        wout_sb = held.tile([P, P], BF16, name="wout_sb")
+        nc.scalar.dma_start(wout_sb[:], wout)
+
+        identity = held.tile([P, P], BF16, name="identity")
+        make_identity(nc, identity[:])
+        flipped = psum.tile([P, S], BF16, name="flipped")
+        for b in range(BLOCKS):
+            nc.tensor.transpose(flipped[:, b * P : (b + 1) * P], rows[:, b, :], identity[:])
+        window = held.tile([P, S], BF16, name="window")
+        nc.vector.tensor_copy(window[:], flipped[:])
+
+        h_ps = psum.tile([P, N], F32, name="h_ps")
+        nc.tensor.matmul(h_ps[:], w_sb[:, 0:P], window[:].indirect(offsets[:]), start=True, stop=True)
+        out_ps = psum.tile([P, N], F32, name="out_ps")
+        nc.tensor.matmul(out_ps[:], w_sb[:, P : 2 * P], window[:].indirect(offsets[:]), start=True, stop=False)
+
+        squares = held.tile([P, R, N], F32, name="squares")
+        nc.scalar.activation(squares[:], hv_sb[:], SQUARE, scale=QUARTER_ROOT)
+        q = held.tile([P, N], F32, name="q")
+        nc.vector.tensor_tensor(q[:], squares[:, 0, :], squares[:, 1, :], ADD)
+        nc.vector.tensor_tensor(q[:], q[:], squares[:, 2, :], ADD)
+        k11q = held.tile([P, N], F32, name="k11q")
+        nc.vector.tensor_tensor(k11q[:], q[:], k11_sb[:], MULT)
+
+        slope = held.tile([P, N], F32, name="slope")
+        nc.vector.scalar_tensor_tensor(slope[:], h_ps[:], INV_SQRT_P, k00_sb[:], MULT, MULT)
+        nc.vector.tensor_tensor(slope[:], slope[:], k1_sb[:], ADD)
+        nc.vector.scalar_tensor_tensor(slope[:], h_ps[:], INV_SQRT_P, slope[:], MULT, MULT)
+        a_bf = held.tile([P, N], BF16, name="a_bf")
+        nc.vector.tensor_tensor(a_bf[:], slope[:], k11q[:], ADD)
+
+        p_ps = psum.tile([P, N], F32, name="p_ps")
+        nc.tensor.matmul(p_ps[:], wprod_sb[:], a_bf[:], start=True, stop=True)
+        p_bf = held.tile([P, N], BF16, name="p_bf")
+        nc.scalar.activation(p_bf[:], p_ps[:], COPY, scale=INV_SQRT_P)
+        nc.tensor.matmul(out_ps[:], wout_sb[:], p_bf[:], start=False, stop=True)
+        out_sb = held.tile([P, N], F32, name="out_sb")
+        nc.scalar.activation(out_sb[:], out_ps[:], COPY, scale=INV_SQRT_P)
+        nc.sync.dma_start(out, out_sb[:])

@@ -8,6 +8,8 @@ S = 1024
 N = 512
 R = 3
 BLOCKS = S // P
+PIECES = 2
+W = N // PIECES
 
 FLOPS = 4 * 2 * P * P * N
 
@@ -21,25 +23,30 @@ SQUARE = mybir.ActivationFunctionType.Square
 
 INV_SQRT_P = 1.0 / math.sqrt(P)
 QUARTER_ROOT = 3.0 ** -0.25
+WARM_UPS = 8
 
 
 def tile_corrproductblock_kernel(tc, table, w, k1, k00, k11, hv, wprod, wout, offs, out):
     nc = tc.nc
-    with tc.tile_pool(name="held", bufs=1) as held, tc.psum_pool(name="psum", bufs=1) as psum:
+    with tc.tile_pool(name="held", bufs=1) as held:
         offsets = held.tile([P, N // 16], U16, name="offsets")
         nc.sync.dma_start(offsets[:], offs)
         rows = held.tile([P, BLOCKS, P], BF16, name="rows")
-        nc.sync.dma_start(rows[:], table.rearrange("(b p) d -> p b d", p=P))
-        w_sb = held.tile([P, 2 * P], BF16, name="w_sb")
-        nc.sync.dma_start(w_sb[:], w)
+        table_blocks = table.rearrange("(b p) d -> p b d", p=P)
+        half = BLOCKS // 2
+        nc.sync.dma_start(rows[:, 0:half, :], table_blocks[:, 0:half, :])
+        nc.sync.dma_start(rows[:, half:BLOCKS, :], table_blocks[:, half:BLOCKS, :])
         hv_sb = held.tile([P, R, N], F32, name="hv_sb")
-        nc.scalar.dma_start(hv_sb[:], hv)
+        for c in range(R):
+            nc.sync.dma_start(hv_sb[:, c, :], hv[:, c, :])
         k11_sb = held.tile([P, N], F32, name="k11_sb")
         nc.sync.dma_start(k11_sb[:], k11)
         k00_sb = held.tile([P, N], F32, name="k00_sb")
         nc.sync.dma_start(k00_sb[:], k00)
         k1_sb = held.tile([P, N], F32, name="k1_sb")
         nc.sync.dma_start(k1_sb[:], k1)
+        w_sb = held.tile([P, 2 * P], BF16, name="w_sb")
+        nc.scalar.dma_start(w_sb[:], w)
         wprod_sb = held.tile([P, P], BF16, name="wprod_sb")
         nc.scalar.dma_start(wprod_sb[:], wprod)
         wout_sb = held.tile([P, P], BF16, name="wout_sb")
@@ -47,37 +54,59 @@ def tile_corrproductblock_kernel(tc, table, w, k1, k00, k11, hv, wprod, wout, of
 
         identity = held.tile([P, P], BF16, name="identity")
         make_identity(nc, identity[:])
-        flipped = psum.tile([P, S], BF16, name="flipped")
-        for b in range(BLOCKS):
-            nc.tensor.transpose(flipped[:, b * P : (b + 1) * P], rows[:, b, :], identity[:])
+
         window = held.tile([P, S], BF16, name="window")
-        nc.vector.tensor_copy(window[:], flipped[:])
+        with tc.psum_pool(name="early_psum", bufs=1) as early_psum:
+            zeros = held.tile([P, N], BF16, name="zeros")
+            nc.vector.memset(zeros[:], 0.0)
+            unread = early_psum.tile([P, N], F32, name="unread")
+            for i in range(WARM_UPS):
+                nc.tensor.matmul(unread[:], zeros[:, 0:P], zeros[:], start=True, stop=True)
+            for g in range(2):
+                flipped = early_psum.tile([P, S // 2], BF16, name=f"flipped{g}")
+                for b in range(half):
+                    nc.tensor.transpose(flipped[:, b * P : (b + 1) * P], rows[:, g * half + b, :], identity[:])
+                nc.vector.tensor_copy(window[:, g * (S // 2) : (g + 1) * (S // 2)], flipped[:])
 
-        h_ps = psum.tile([P, N], F32, name="h_ps")
-        nc.tensor.matmul(h_ps[:], w_sb[:, 0:P], window[:].indirect(offsets[:]), start=True, stop=True)
-        out_ps = psum.tile([P, N], F32, name="out_ps")
-        nc.tensor.matmul(out_ps[:], w_sb[:, P : 2 * P], window[:].indirect(offsets[:]), start=True, stop=False)
+        with tc.psum_pool(name="psum", bufs=1) as psum:
+            piece_offsets = [offsets[:, j * (W // 16) : (j + 1) * (W // 16)] for j in range(PIECES)]
+            h_ps = [psum.tile([P, W], F32, name=f"h_ps{j}") for j in range(PIECES)]
+            out_ps = [psum.tile([P, W], F32, name=f"out_ps{j}") for j in range(PIECES)]
+            p_ps = [psum.tile([P, W], F32, name=f"p_ps{j}") for j in range(PIECES)]
+            for j in range(PIECES):
+                nc.tensor.matmul(h_ps[j][:], w_sb[:, 0:P], window[:].indirect(piece_offsets[j]), start=True, stop=True)
+            for j in range(PIECES):
+                nc.tensor.matmul(
+                    out_ps[j][:], w_sb[:, P : 2 * P], window[:].indirect(piece_offsets[j]), start=True, stop=False
+                )
 
-        squares = held.tile([P, R, N], F32, name="squares")
-        nc.scalar.activation(squares[:], hv_sb[:], SQUARE, scale=QUARTER_ROOT)
-        q = held.tile([P, N], F32, name="q")
-        nc.vector.tensor_tensor(q[:], squares[:, 0, :], squares[:, 1, :], ADD)
-        nc.vector.tensor_tensor(q[:], q[:], squares[:, 2, :], ADD)
-        k11q = held.tile([P, N], F32, name="k11q")
-        nc.vector.tensor_tensor(k11q[:], q[:], k11_sb[:], MULT)
+            squares = held.tile([P, R, N], F32, name="squares")
+            for c in range(R):
+                nc.scalar.activation(squares[:, c, :], hv_sb[:, c, :], SQUARE, scale=QUARTER_ROOT)
+            k11q = held.tile([P, N], F32, name="k11q")
+            nc.vector.tensor_tensor(k11q[:], squares[:, 0, :], squares[:, 1, :], ADD)
+            nc.vector.tensor_tensor(k11q[:], k11q[:], squares[:, 2, :], ADD)
+            nc.vector.tensor_tensor(k11q[:], k11q[:], k11_sb[:], MULT)
 
-        slope = held.tile([P, N], F32, name="slope")
-        nc.vector.scalar_tensor_tensor(slope[:], h_ps[:], INV_SQRT_P, k00_sb[:], MULT, MULT)
-        nc.vector.tensor_tensor(slope[:], slope[:], k1_sb[:], ADD)
-        nc.vector.scalar_tensor_tensor(slope[:], h_ps[:], INV_SQRT_P, slope[:], MULT, MULT)
-        a_bf = held.tile([P, N], BF16, name="a_bf")
-        nc.vector.tensor_tensor(a_bf[:], slope[:], k11q[:], ADD)
+            for j in range(PIECES):
+                cols = slice(j * W, (j + 1) * W)
+                slope = held.tile([P, W], F32, name=f"slope{j}")
+                nc.vector.scalar_tensor_tensor(slope[:], h_ps[j][:], INV_SQRT_P, k00_sb[:, cols], MULT, MULT)
+                nc.vector.tensor_tensor(slope[:], slope[:], k1_sb[:, cols], ADD)
+                nc.vector.scalar_tensor_tensor(slope[:], h_ps[j][:], INV_SQRT_P, slope[:], MULT, MULT)
+                a_bf = held.tile([P, W], BF16, name=f"a_bf{j}")
+                nc.vector.tensor_tensor(a_bf[:], slope[:], k11q[:, cols], ADD)
 
-        p_ps = psum.tile([P, N], F32, name="p_ps")
-        nc.tensor.matmul(p_ps[:], wprod_sb[:], a_bf[:], start=True, stop=True)
-        p_bf = held.tile([P, N], BF16, name="p_bf")
-        nc.scalar.activation(p_bf[:], p_ps[:], COPY, scale=INV_SQRT_P)
-        nc.tensor.matmul(out_ps[:], wout_sb[:], p_bf[:], start=False, stop=True)
-        out_sb = held.tile([P, N], F32, name="out_sb")
-        nc.scalar.activation(out_sb[:], out_ps[:], COPY, scale=INV_SQRT_P)
-        nc.sync.dma_start(out, out_sb[:])
+                nc.tensor.matmul(p_ps[j][:], wprod_sb[:], a_bf[:], start=True, stop=True)
+                p_bf = held.tile([P, W], BF16, name=f"p_bf{j}")
+                out_sb = held.tile([P, W], F32, name=f"out_sb{j}")
+                if j == 0:
+                    nc.scalar.activation(p_bf[:], p_ps[j][:], COPY, scale=INV_SQRT_P)
+                else:
+                    nc.vector.tensor_scalar_mul(p_bf[:], p_ps[j][:], INV_SQRT_P)
+                nc.tensor.matmul(out_ps[j][:], wout_sb[:], p_bf[:], start=False, stop=True)
+                if j == 0:
+                    nc.scalar.activation(out_sb[:], out_ps[j][:], COPY, scale=INV_SQRT_P)
+                else:
+                    nc.vector.tensor_scalar_mul(out_sb[:], out_ps[j][:], INV_SQRT_P)
+                nc.sync.dma_start(out[:, cols], out_sb[:])

@@ -23,7 +23,6 @@ SQUARE = mybir.ActivationFunctionType.Square
 
 INV_SQRT_P = 1.0 / math.sqrt(P)
 QUARTER_ROOT = 3.0 ** -0.25
-WARM_UPS = 8
 
 
 def tile_corrproductblock_kernel(tc, table, w, k1, k00, k11, hv, wprod, wout, offs, out):
@@ -57,11 +56,6 @@ def tile_corrproductblock_kernel(tc, table, w, k1, k00, k11, hv, wprod, wout, of
 
         window = held.tile([P, S], BF16, name="window")
         with tc.psum_pool(name="early_psum", bufs=1) as early_psum:
-            zeros = held.tile([P, N], BF16, name="zeros")
-            nc.vector.memset(zeros[:], 0.0)
-            unread = early_psum.tile([P, N], F32, name="unread")
-            for i in range(WARM_UPS):
-                nc.tensor.matmul(unread[:], zeros[:, 0:P], zeros[:], start=True, stop=True)
             for g in range(2):
                 flipped = early_psum.tile([P, S // 2], BF16, name=f"flipped{g}")
                 for b in range(half):

@@ -7,8 +7,10 @@ P = 128
 S = 1024
 N = 512
 R = 3
-BLOCKS = S // P
-PIECES = 2
+HALVES = 2
+RUN = S // (HALVES * P)
+H = N // HALVES
+PIECES = 4
 W = N // PIECES
 
 FLOPS = 4 * 2 * P * P * N
@@ -27,14 +29,19 @@ QUARTER_ROOT = 3.0 ** -0.25
 
 def tile_corrproductblock_kernel(tc, table, w, k1, k00, k11, hv, wprod, wout, offs, out):
     nc = tc.nc
-    with tc.tile_pool(name="held", bufs=1) as held:
+    with tc.tile_pool(name="held", bufs=1) as held, tc.tile_pool(name="work", bufs=PIECES) as work:
         offsets = held.tile([P, N // 16], U16, name="offsets")
         nc.sync.dma_start(offsets[:], offs)
-        rows = held.tile([P, BLOCKS, P], BF16, name="rows")
-        table_blocks = table.rearrange("(b p) d -> p b d", p=P)
-        half = BLOCKS // 2
-        nc.sync.dma_start(rows[:, 0:half, :], table_blocks[:, 0:half, :])
-        nc.sync.dma_start(rows[:, half:BLOCKS, :], table_blocks[:, half:BLOCKS, :])
+        rows = held.tile([P, HALVES, RUN, P], BF16, name="rows")
+        table_runs = table.rearrange("(g p b) d -> p g b d", g=HALVES, p=P, b=RUN)
+        for g in range(HALVES):
+            nc.sync.dma_start(rows[:, g, :, :], table_runs[:, g, :, :])
+        w_sb = held.tile([P, 2 * P], BF16, name="w_sb")
+        nc.sync.dma_start(w_sb[:], w)
+        wprod_sb = held.tile([P, P], BF16, name="wprod_sb")
+        nc.sync.dma_start(wprod_sb[:], wprod)
+        wout_sb = held.tile([P, P], BF16, name="wout_sb")
+        nc.sync.dma_start(wout_sb[:], wout)
         hv_sb = held.tile([P, R, N], F32, name="hv_sb")
         for c in range(R):
             nc.sync.dma_start(hv_sb[:, c, :], hv[:, c, :])
@@ -44,62 +51,74 @@ def tile_corrproductblock_kernel(tc, table, w, k1, k00, k11, hv, wprod, wout, of
         nc.sync.dma_start(k00_sb[:], k00)
         k1_sb = held.tile([P, N], F32, name="k1_sb")
         nc.sync.dma_start(k1_sb[:], k1)
-        w_sb = held.tile([P, 2 * P], BF16, name="w_sb")
-        nc.scalar.dma_start(w_sb[:], w)
-        wprod_sb = held.tile([P, P], BF16, name="wprod_sb")
-        nc.scalar.dma_start(wprod_sb[:], wprod)
-        wout_sb = held.tile([P, P], BF16, name="wout_sb")
-        nc.scalar.dma_start(wout_sb[:], wout)
 
         identity = held.tile([P, P], BF16, name="identity")
         make_identity(nc, identity[:])
 
         window = held.tile([P, S], BF16, name="window")
         with tc.psum_pool(name="early_psum", bufs=1) as early_psum:
-            for g in range(2):
-                flipped = early_psum.tile([P, S // 2], BF16, name=f"flipped{g}")
-                for b in range(half):
-                    nc.tensor.transpose(flipped[:, b * P : (b + 1) * P], rows[:, g * half + b, :], identity[:])
-                nc.vector.tensor_copy(window[:, g * (S // 2) : (g + 1) * (S // 2)], flipped[:])
+            for g in range(HALVES):
+                flipped = early_psum.tile([P, RUN, P], BF16, name=f"flipped{g}")
+                for b in range(RUN):
+                    nc.tensor.transpose(flipped[:, b, :], rows[:, g, b, :], identity[:])
+                nc.vector.tensor_copy(
+                    window[:, g * (S // HALVES) : (g + 1) * (S // HALVES)].rearrange("d (p b) -> d p b", b=RUN),
+                    flipped[:].rearrange("d b p -> d p b"),
+                )
 
-        with tc.psum_pool(name="psum", bufs=1) as psum:
-            piece_offsets = [offsets[:, j * (W // 16) : (j + 1) * (W // 16)] for j in range(PIECES)]
-            h_ps = [psum.tile([P, W], F32, name=f"h_ps{j}") for j in range(PIECES)]
+        with tc.psum_pool(name="psum", bufs=1) as psum, tc.psum_pool(name="p_psum", bufs=2) as p_psum:
+            h_ps = [psum.tile([P, H], F32, name=f"h_ps{g}") for g in range(HALVES)]
+            for g in range(HALVES):
+                nc.tensor.matmul(
+                    h_ps[g][:],
+                    w_sb[:, 0:P],
+                    window[:].indirect(offsets[:, g * (H // 16) : (g + 1) * (H // 16)]),
+                    start=True,
+                    stop=True,
+                )
             out_ps = [psum.tile([P, W], F32, name=f"out_ps{j}") for j in range(PIECES)]
-            p_ps = [psum.tile([P, W], F32, name=f"p_ps{j}") for j in range(PIECES)]
-            for j in range(PIECES):
-                nc.tensor.matmul(h_ps[j][:], w_sb[:, 0:P], window[:].indirect(piece_offsets[j]), start=True, stop=True)
             for j in range(PIECES):
                 nc.tensor.matmul(
-                    out_ps[j][:], w_sb[:, P : 2 * P], window[:].indirect(piece_offsets[j]), start=True, stop=False
+                    out_ps[j][:],
+                    w_sb[:, P : 2 * P],
+                    window[:].indirect(offsets[:, j * (W // 16) : (j + 1) * (W // 16)]),
+                    start=True,
+                    stop=False,
                 )
 
             squares = held.tile([P, R, N], F32, name="squares")
             for c in range(R):
                 nc.scalar.activation(squares[:, c, :], hv_sb[:, c, :], SQUARE, scale=QUARTER_ROOT)
+            halves = [slice(g * H, (g + 1) * H) for g in range(HALVES)]
             k11q = held.tile([P, N], F32, name="k11q")
-            nc.vector.tensor_tensor(k11q[:], squares[:, 0, :], squares[:, 1, :], ADD)
-            nc.vector.tensor_tensor(k11q[:], k11q[:], squares[:, 2, :], ADD)
-            nc.vector.tensor_tensor(k11q[:], k11q[:], k11_sb[:], MULT)
+            for cols in halves:
+                nc.vector.tensor_tensor(k11q[:, cols], squares[:, 0, cols], squares[:, 1, cols], ADD)
+            for cols in halves:
+                nc.vector.tensor_tensor(k11q[:, cols], k11q[:, cols], squares[:, 2, cols], ADD)
+            for cols in halves:
+                nc.vector.tensor_tensor(k11q[:, cols], k11q[:, cols], k11_sb[:, cols], MULT)
+            slope = held.tile([P, N], F32, name="slope")
+            for g, cols in enumerate(halves):
+                nc.vector.scalar_tensor_tensor(slope[:, cols], h_ps[g][:], INV_SQRT_P, k00_sb[:, cols], MULT, MULT)
+            for cols in halves:
+                nc.vector.tensor_tensor(slope[:, cols], slope[:, cols], k1_sb[:, cols], ADD)
+            for g, cols in enumerate(halves):
+                nc.vector.scalar_tensor_tensor(slope[:, cols], h_ps[g][:], INV_SQRT_P, slope[:, cols], MULT, MULT)
 
             for j in range(PIECES):
                 cols = slice(j * W, (j + 1) * W)
-                slope = held.tile([P, W], F32, name=f"slope{j}")
-                nc.vector.scalar_tensor_tensor(slope[:], h_ps[j][:], INV_SQRT_P, k00_sb[:, cols], MULT, MULT)
-                nc.vector.tensor_tensor(slope[:], slope[:], k1_sb[:, cols], ADD)
-                nc.vector.scalar_tensor_tensor(slope[:], h_ps[j][:], INV_SQRT_P, slope[:], MULT, MULT)
-                a_bf = held.tile([P, W], BF16, name=f"a_bf{j}")
-                nc.vector.tensor_tensor(a_bf[:], slope[:], k11q[:, cols], ADD)
-
-                nc.tensor.matmul(p_ps[j][:], wprod_sb[:], a_bf[:], start=True, stop=True)
-                p_bf = held.tile([P, W], BF16, name=f"p_bf{j}")
-                out_sb = held.tile([P, W], F32, name=f"out_sb{j}")
-                if j == 0:
-                    nc.scalar.activation(p_bf[:], p_ps[j][:], COPY, scale=INV_SQRT_P)
+                a_bf = work.tile([P, W], BF16, name="a_bf")
+                nc.vector.tensor_tensor(a_bf[:], slope[:, cols], k11q[:, cols], ADD)
+                p_ps = p_psum.tile([P, W], F32, name="p_ps")
+                nc.tensor.matmul(p_ps[:], wprod_sb[:], a_bf[:], start=True, stop=True)
+                p_bf = work.tile([P, W], BF16, name="p_bf")
+                out_sb = work.tile([P, W], F32, name="out_sb")
+                if j < 2:
+                    nc.scalar.activation(p_bf[:], p_ps[:], COPY, scale=INV_SQRT_P)
                 else:
-                    nc.vector.tensor_scalar_mul(p_bf[:], p_ps[j][:], INV_SQRT_P)
+                    nc.vector.tensor_scalar_mul(p_bf[:], p_ps[:], INV_SQRT_P)
                 nc.tensor.matmul(out_ps[j][:], wout_sb[:], p_bf[:], start=False, stop=True)
-                if j == 0:
+                if j < 2:
                     nc.scalar.activation(out_sb[:], out_ps[j][:], COPY, scale=INV_SQRT_P)
                 else:
                     nc.vector.tensor_scalar_mul(out_sb[:], out_ps[j][:], INV_SQRT_P)

@@ -45,12 +45,12 @@ def tile_corrproductblock_kernel(tc, table, w, k1, k00, k11, hv, wprod, wout, of
         hv_sb = held.tile([P, R, N], F32, name="hv_sb")
         for c in range(R):
             nc.sync.dma_start(hv_sb[:, c, :], hv[:, c, :])
-        k11_sb = held.tile([P, N], F32, name="k11_sb")
-        nc.sync.dma_start(k11_sb[:], k11)
         k00_sb = held.tile([P, N], F32, name="k00_sb")
         nc.sync.dma_start(k00_sb[:], k00)
         k1_sb = held.tile([P, N], F32, name="k1_sb")
         nc.sync.dma_start(k1_sb[:], k1)
+        k11_sb = held.tile([P, N], F32, name="k11_sb")
+        nc.sync.dma_start(k11_sb[:], k11)
 
         identity = held.tile([P, P], BF16, name="identity")
         make_identity(nc, identity[:])
@@ -90,16 +90,18 @@ def tile_corrproductblock_kernel(tc, table, w, k1, k00, k11, hv, wprod, wout, of
             for c in range(R):
                 nc.scalar.activation(squares[:, c, :], hv_sb[:, c, :], SQUARE, scale=QUARTER_ROOT)
             halves = [slice(g * H, (g + 1) * H) for g in range(HALVES)]
+            q = held.tile([P, N], F32, name="q")
+            slope = held.tile([P, N], F32, name="slope")
             k11q = held.tile([P, N], F32, name="k11q")
             for cols in halves:
-                nc.vector.tensor_tensor(k11q[:, cols], squares[:, 0, cols], squares[:, 1, cols], ADD)
-            for cols in halves:
-                nc.vector.tensor_tensor(k11q[:, cols], k11q[:, cols], squares[:, 2, cols], ADD)
-            for cols in halves:
-                nc.vector.tensor_tensor(k11q[:, cols], k11q[:, cols], k11_sb[:, cols], MULT)
-            slope = held.tile([P, N], F32, name="slope")
+                nc.vector.tensor_tensor(q[:, cols], squares[:, 0, cols], squares[:, 1, cols], ADD)
             for g, cols in enumerate(halves):
                 nc.vector.scalar_tensor_tensor(slope[:, cols], h_ps[g][:], INV_SQRT_P, k00_sb[:, cols], MULT, MULT)
+            for cols in halves:
+                nc.vector.tensor_tensor(q[:, cols], q[:, cols], squares[:, 2, cols], ADD)
+            for j in range(PIECES):
+                cols = slice(j * W, (j + 1) * W)
+                nc.gpsimd.tensor_tensor(k11q[:, cols], q[:, cols], k11_sb[:, cols], MULT)
             for cols in halves:
                 nc.vector.tensor_tensor(slope[:, cols], slope[:, cols], k1_sb[:, cols], ADD)
             for g, cols in enumerate(halves):

@@ -32,25 +32,25 @@ def tile_corrproductblock_kernel(tc, table, w, k1, k00, k11, hv, wprod, wout, of
     with tc.tile_pool(name="held", bufs=1) as held, tc.tile_pool(name="work", bufs=PIECES) as work:
         offsets = held.tile([P, N // 16], U16, name="offsets")
         nc.sync.dma_start(offsets[:], offs)
-        rows = held.tile([P, HALVES, RUN, P], BF16, name="rows")
+        rows = held.tile([P, HALVES, RUN, P], BF16, name="rows", tag="rows_then_q")
         table_runs = table.rearrange("(g p b) d -> p g b d", g=HALVES, p=P, b=RUN)
         for g in range(HALVES):
             nc.sync.dma_start(rows[:, g, :, :], table_runs[:, g, :, :])
         w_sb = held.tile([P, 2 * P], BF16, name="w_sb")
         nc.sync.dma_start(w_sb[:], w)
-        wprod_sb = held.tile([P, P], BF16, name="wprod_sb")
-        nc.sync.dma_start(wprod_sb[:], wprod)
-        wout_sb = held.tile([P, P], BF16, name="wout_sb")
-        nc.sync.dma_start(wout_sb[:], wout)
         hv_sb = held.tile([P, R, N], F32, name="hv_sb")
         for c in range(R):
             nc.sync.dma_start(hv_sb[:, c, :], hv[:, c, :])
+        k11_sb = held.tile([P, N], F32, name="k11_sb")
+        nc.sync.dma_start(k11_sb[:], k11)
         k00_sb = held.tile([P, N], F32, name="k00_sb")
         nc.sync.dma_start(k00_sb[:], k00)
         k1_sb = held.tile([P, N], F32, name="k1_sb")
         nc.sync.dma_start(k1_sb[:], k1)
-        k11_sb = held.tile([P, N], F32, name="k11_sb")
-        nc.sync.dma_start(k11_sb[:], k11)
+        wprod_sb = held.tile([P, P], BF16, name="wprod_sb")
+        nc.sync.dma_start(wprod_sb[:], wprod)
+        wout_sb = held.tile([P, P], BF16, name="wout_sb")
+        nc.sync.dma_start(wout_sb[:], wout)
 
         identity = held.tile([P, P], BF16, name="identity")
         make_identity(nc, identity[:])
@@ -90,38 +90,36 @@ def tile_corrproductblock_kernel(tc, table, w, k1, k00, k11, hv, wprod, wout, of
             for c in range(R):
                 nc.scalar.activation(squares[:, c, :], hv_sb[:, c, :], SQUARE, scale=QUARTER_ROOT)
             halves = [slice(g * H, (g + 1) * H) for g in range(HALVES)]
-            q = held.tile([P, N], F32, name="q")
+            q = held.tile([P, N], F32, name="q", tag="rows_then_q")
             slope = held.tile([P, N], F32, name="slope")
             k11q = held.tile([P, N], F32, name="k11q")
             for cols in halves:
                 nc.vector.tensor_tensor(q[:, cols], squares[:, 0, cols], squares[:, 1, cols], ADD)
-            for g, cols in enumerate(halves):
-                nc.vector.scalar_tensor_tensor(slope[:, cols], h_ps[g][:], INV_SQRT_P, k00_sb[:, cols], MULT, MULT)
             for cols in halves:
                 nc.vector.tensor_tensor(q[:, cols], q[:, cols], squares[:, 2, cols], ADD)
             for j in range(PIECES):
                 cols = slice(j * W, (j + 1) * W)
                 nc.gpsimd.tensor_tensor(k11q[:, cols], q[:, cols], k11_sb[:, cols], MULT)
+            for g, cols in enumerate(halves):
+                nc.vector.scalar_tensor_tensor(slope[:, cols], h_ps[g][:], INV_SQRT_P, k00_sb[:, cols], MULT, MULT)
             for cols in halves:
                 nc.vector.tensor_tensor(slope[:, cols], slope[:, cols], k1_sb[:, cols], ADD)
             for g, cols in enumerate(halves):
                 nc.vector.scalar_tensor_tensor(slope[:, cols], h_ps[g][:], INV_SQRT_P, slope[:, cols], MULT, MULT)
 
+            pieces = [slice(j * W, (j + 1) * W) for j in range(PIECES)]
+            p_ps = {}
+            for step in range(PIECES + 1):
+                if step < PIECES:
+                    a_bf = work.tile([P, W], BF16, name="a_bf")
+                    nc.vector.tensor_tensor(a_bf[:], slope[:, pieces[step]], k11q[:, pieces[step]], ADD)
+                    p_ps[step] = p_psum.tile([P, W], F32, name="p_ps")
+                    nc.tensor.matmul(p_ps[step][:], wprod_sb[:], a_bf[:], start=True, stop=True)
+                if step > 0:
+                    p_bf = work.tile([P, W], BF16, name="p_bf")
+                    nc.scalar.activation(p_bf[:], p_ps[step - 1][:], COPY, scale=INV_SQRT_P)
+                    nc.tensor.matmul(out_ps[step - 1][:], wout_sb[:], p_bf[:], start=False, stop=True)
             for j in range(PIECES):
-                cols = slice(j * W, (j + 1) * W)
-                a_bf = work.tile([P, W], BF16, name="a_bf")
-                nc.vector.tensor_tensor(a_bf[:], slope[:, cols], k11q[:, cols], ADD)
-                p_ps = p_psum.tile([P, W], F32, name="p_ps")
-                nc.tensor.matmul(p_ps[:], wprod_sb[:], a_bf[:], start=True, stop=True)
-                p_bf = work.tile([P, W], BF16, name="p_bf")
                 out_sb = work.tile([P, W], F32, name="out_sb")
-                if j < 2:
-                    nc.scalar.activation(p_bf[:], p_ps[:], COPY, scale=INV_SQRT_P)
-                else:
-                    nc.vector.tensor_scalar_mul(p_bf[:], p_ps[:], INV_SQRT_P)
-                nc.tensor.matmul(out_ps[j][:], wout_sb[:], p_bf[:], start=False, stop=True)
-                if j < 2:
-                    nc.scalar.activation(out_sb[:], out_ps[j][:], COPY, scale=INV_SQRT_P)
-                else:
-                    nc.vector.tensor_scalar_mul(out_sb[:], out_ps[j][:], INV_SQRT_P)
-                nc.sync.dma_start(out[:, cols], out_sb[:])
+                nc.vector.tensor_scalar_mul(out_sb[:], out_ps[j][:], INV_SQRT_P)
+                nc.sync.dma_start(out[:, pieces[j]], out_sb[:])

@@ -9,6 +9,7 @@ N = 512
 R = 3
 HALVES = 2
 RUN = S // (HALVES * P)
+PAIR = 2
 H = N // HALVES
 PIECES = 4
 W = N // PIECES
@@ -30,12 +31,12 @@ QUARTER_ROOT = 3.0 ** -0.25
 def tile_corrproductblock_kernel(tc, table, w, k1, k00, k11, hv, wprod, wout, offs, out):
     nc = tc.nc
     with tc.tile_pool(name="held", bufs=1) as held, tc.tile_pool(name="work", bufs=PIECES) as work:
-        offsets = held.tile([P, N // 16], U16, name="offsets")
-        nc.sync.dma_start(offsets[:], offs)
         rows = held.tile([P, HALVES, RUN, P], BF16, name="rows", tag="rows_then_q")
         table_runs = table.rearrange("(g p b) d -> p g b d", g=HALVES, p=P, b=RUN)
         for g in range(HALVES):
             nc.sync.dma_start(rows[:, g, :, :], table_runs[:, g, :, :])
+        offsets = held.tile([P, N // 16], U16, name="offsets")
+        nc.sync.dma_start(offsets[:], offs)
         w_sb = held.tile([P, 2 * P], BF16, name="w_sb")
         nc.sync.dma_start(w_sb[:], w)
         hv_sb = held.tile([P, R, N], F32, name="hv_sb")
@@ -56,15 +57,16 @@ def tile_corrproductblock_kernel(tc, table, w, k1, k00, k11, hv, wprod, wout, of
         make_identity(nc, identity[:])
 
         window = held.tile([P, S], BF16, name="window")
+        window_runs = window[:].rearrange("d (g p b) -> d g p b", g=HALVES, p=P, b=RUN)
         with tc.psum_pool(name="early_psum", bufs=1) as early_psum:
             for g in range(HALVES):
-                flipped = early_psum.tile([P, RUN, P], BF16, name=f"flipped{g}")
-                for b in range(RUN):
-                    nc.tensor.transpose(flipped[:, b, :], rows[:, g, b, :], identity[:])
-                nc.vector.tensor_copy(
-                    window[:, g * (S // HALVES) : (g + 1) * (S // HALVES)].rearrange("d (p b) -> d p b", b=RUN),
-                    flipped[:].rearrange("d b p -> d p b"),
-                )
+                for first in range(0, RUN, PAIR):
+                    flipped = early_psum.tile([P, PAIR, P], BF16, name=f"flipped{g}{first}")
+                    for b in range(PAIR):
+                        nc.tensor.transpose(flipped[:, b, :], rows[:, g, first + b, :], identity[:])
+                    nc.vector.tensor_copy(
+                        window_runs[:, g, :, first : first + PAIR], flipped[:].rearrange("d b p -> d p b")
+                    )
 
         with tc.psum_pool(name="psum", bufs=1) as psum, tc.psum_pool(name="p_psum", bufs=2) as p_psum:
             h_ps = [psum.tile([P, H], F32, name=f"h_ps{g}") for g in range(HALVES)]
@@ -97,8 +99,7 @@ def tile_corrproductblock_kernel(tc, table, w, k1, k00, k11, hv, wprod, wout, of
                 nc.vector.tensor_tensor(q[:, cols], squares[:, 0, cols], squares[:, 1, cols], ADD)
             for cols in halves:
                 nc.vector.tensor_tensor(q[:, cols], q[:, cols], squares[:, 2, cols], ADD)
-            for j in range(PIECES):
-                cols = slice(j * W, (j + 1) * W)
+            for cols in halves:
                 nc.gpsimd.tensor_tensor(k11q[:, cols], q[:, cols], k11_sb[:, cols], MULT)
             for g, cols in enumerate(halves):
                 nc.vector.scalar_tensor_tensor(slope[:, cols], h_ps[g][:], INV_SQRT_P, k00_sb[:, cols], MULT, MULT)

@@ -118,9 +118,15 @@ def tile_corrproductblock_kernel(tc, table, w, k1, k00, k11, hv, wprod, wout, of
                     nc.tensor.matmul(p_ps[step][:], wprod_sb[:], a_bf[:], start=True, stop=True)
                 if step > 0:
                     p_bf = work.tile([P, W], BF16, name="p_bf")
-                    nc.scalar.activation(p_bf[:], p_ps[step - 1][:], COPY, scale=INV_SQRT_P)
+                    if step - 1 < PIECES // 2:
+                        nc.scalar.activation(p_bf[:], p_ps[step - 1][:], COPY, scale=INV_SQRT_P)
+                    else:
+                        nc.vector.tensor_scalar_mul(p_bf[:], p_ps[step - 1][:], INV_SQRT_P)
                     nc.tensor.matmul(out_ps[step - 1][:], wout_sb[:], p_bf[:], start=False, stop=True)
             for j in range(PIECES):
                 out_sb = work.tile([P, W], F32, name="out_sb")
-                nc.vector.tensor_scalar_mul(out_sb[:], out_ps[j][:], INV_SQRT_P)
+                if j < PIECES // 2:
+                    nc.scalar.activation(out_sb[:], out_ps[j][:], COPY, scale=INV_SQRT_P)
+                else:
+                    nc.vector.tensor_scalar_mul(out_sb[:], out_ps[j][:], INV_SQRT_P)
                 nc.sync.dma_start(out[:, pieces[j]], out_sb[:])

@@ -68,8 +68,8 @@ def tile_corrproductblock_kernel(tc, table, w, k1, k00, k11, hv, wprod, wout, of
                         window_runs[:, g, :, first : first + PAIR], flipped[:].rearrange("d b p -> d p b")
                     )
 
-        with tc.psum_pool(name="psum", bufs=1) as psum, tc.psum_pool(name="p_psum", bufs=2) as p_psum:
-            h_ps = [psum.tile([P, H], F32, name=f"h_ps{g}") for g in range(HALVES)]
+        with tc.psum_pool(name="psum", bufs=1) as psum:
+            h_ps = [psum.tile([P, H], F32, name=f"h_ps{g}", tag=f"p_bank{PIECES - HALVES + g}") for g in range(HALVES)]
             for g in range(HALVES):
                 nc.tensor.matmul(
                     h_ps[g][:],
@@ -114,7 +114,7 @@ def tile_corrproductblock_kernel(tc, table, w, k1, k00, k11, hv, wprod, wout, of
                 if step < PIECES:
                     a_bf = work.tile([P, W], BF16, name="a_bf")
                     nc.vector.tensor_tensor(a_bf[:], slope[:, pieces[step]], k11q[:, pieces[step]], ADD)
-                    p_ps[step] = p_psum.tile([P, W], F32, name="p_ps")
+                    p_ps[step] = psum.tile([P, W], F32, name=f"p_ps{step}", tag=f"p_bank{step}")
                     nc.tensor.matmul(p_ps[step][:], wprod_sb[:], a_bf[:], start=True, stop=True)
                 if step > 0:
                     p_bf = work.tile([P, W], BF16, name="p_bf")

@@ -129,4 +129,5 @@ def tile_corrproductblock_kernel(tc, table, w, k1, k00, k11, hv, wprod, wout, of
                     nc.scalar.activation(out_sb[:], out_ps[j][:], COPY, scale=INV_SQRT_P)
                 else:
                     nc.vector.tensor_scalar_mul(out_sb[:], out_ps[j][:], INV_SQRT_P)
-                nc.sync.dma_start(out[:, pieces[j]], out_sb[:])
+                queue = nc.scalar if j < PIECES // 2 else nc.sync
+                queue.dma_start(out[:, pieces[j]], out_sb[:])

@@ -25,23 +25,24 @@ COPY = mybir.ActivationFunctionType.Copy
 SQUARE = mybir.ActivationFunctionType.Square
 
 INV_SQRT_P = 1.0 / math.sqrt(P)
-QUARTER_ROOT = 3.0 ** -0.25
+INV_SQRT_R = 1.0 / math.sqrt(R)
 
 
 def tile_corrproductblock_kernel(tc, table, w, k1, k00, k11, hv, wprod, wout, offs, out):
     nc = tc.nc
     with tc.tile_pool(name="held", bufs=1) as held, tc.tile_pool(name="work", bufs=PIECES) as work:
-        rows = held.tile([P, HALVES, RUN, P], BF16, name="rows", tag="rows_then_q")
+        rows = [held.tile([P, RUN, P], BF16, name=f"rows{g}", tag=f"rows{g}_and_later") for g in range(HALVES)]
         table_runs = table.rearrange("(g p b) d -> p g b d", g=HALVES, p=P, b=RUN)
         for g in range(HALVES):
-            nc.sync.dma_start(rows[:, g, :, :], table_runs[:, g, :, :])
+            nc.sync.dma_start(rows[g][:], table_runs[:, g, :, :])
+        hv_sb = held.tile([P, R, N], F32, name="hv_sb")
+        for c in range(R - 1):
+            nc.sync.dma_start(hv_sb[:, c, :], hv[:, c, :])
         offsets = held.tile([P, N // 16], U16, name="offsets")
         nc.sync.dma_start(offsets[:], offs)
         w_sb = held.tile([P, 2 * P], BF16, name="w_sb")
         nc.sync.dma_start(w_sb[:], w)
-        hv_sb = held.tile([P, R, N], F32, name="hv_sb")
-        for c in range(R):
-            nc.sync.dma_start(hv_sb[:, c, :], hv[:, c, :])
+        nc.sync.dma_start(hv_sb[:, R - 1, :], hv[:, R - 1, :])
         k11_sb = held.tile([P, N], F32, name="k11_sb")
         nc.sync.dma_start(k11_sb[:], k11)
         k00_sb = held.tile([P, N], F32, name="k00_sb")
@@ -53,7 +54,7 @@ def tile_corrproductblock_kernel(tc, table, w, k1, k00, k11, hv, wprod, wout, of
         wout_sb = held.tile([P, P], BF16, name="wout_sb")
         nc.sync.dma_start(wout_sb[:], wout)
 
-        identity = held.tile([P, P], BF16, name="identity")
+        identity = held.tile([P, P], BF16, name="identity", tag="identity_and_later")
         make_identity(nc, identity[:])
 
         window = held.tile([P, S], BF16, name="window")
@@ -63,10 +64,12 @@ def tile_corrproductblock_kernel(tc, table, w, k1, k00, k11, hv, wprod, wout, of
                 for first in range(0, RUN, PAIR):
                     flipped = early_psum.tile([P, PAIR, P], BF16, name=f"flipped{g}{first}")
                     for b in range(PAIR):
-                        nc.tensor.transpose(flipped[:, b, :], rows[:, g, first + b, :], identity[:])
-                    nc.vector.tensor_copy(
-                        window_runs[:, g, :, first : first + PAIR], flipped[:].rearrange("d b p -> d p b")
-                    )
+                        nc.tensor.transpose(flipped[:, b, :], rows[g][:, first + b, :], identity[:])
+                    columns = window_runs[:, g, :, first : first + PAIR]
+                    if first == 0:
+                        nc.scalar.copy(columns, flipped[:].rearrange("d b p -> d p b"))
+                    else:
+                        nc.vector.tensor_copy(columns, flipped[:].rearrange("d b p -> d p b"))
 
         with tc.psum_pool(name="psum", bufs=1) as psum:
             h_ps = [psum.tile([P, H], F32, name=f"h_ps{g}", tag=f"p_bank{PIECES - HALVES + g}") for g in range(HALVES)]
@@ -88,32 +91,41 @@ def tile_corrproductblock_kernel(tc, table, w, k1, k00, k11, hv, wprod, wout, of
                     stop=False,
                 )
 
-            squares = held.tile([P, R, N], F32, name="squares")
-            for c in range(R):
-                nc.scalar.activation(squares[:, c, :], hv_sb[:, c, :], SQUARE, scale=QUARTER_ROOT)
             halves = [slice(g * H, (g + 1) * H) for g in range(HALVES)]
-            q = held.tile([P, N], F32, name="q", tag="rows_then_q")
-            slope = held.tile([P, N], F32, name="slope")
+            tags = ["rows1_and_later", "identity_and_later"]
+            squares = [held.tile([P, R, H], F32, name=f"squares{g}", tag=tags[g]) for g in range(HALVES)]
+            early_square = held.tile([P, H], F32, name="early_square")
+            first_squares = [early_square[:], squares[1][:, 0, :]]
+            for g, engine in enumerate((nc.gpsimd, nc.vector)):
+                engine.tensor_tensor(first_squares[g], hv_sb[:, 0, halves[g]], hv_sb[:, 0, halves[g]], MULT)
+            for c in range(1, R):
+                for g, cols in enumerate(halves):
+                    nc.scalar.activation(squares[g][:, c, :], hv_sb[:, c, cols], SQUARE)
+            q = held.tile([P, N], F32, name="q")
             k11q = held.tile([P, N], F32, name="k11q")
-            for cols in halves:
-                nc.vector.tensor_tensor(q[:, cols], squares[:, 0, cols], squares[:, 1, cols], ADD)
-            for cols in halves:
-                nc.vector.tensor_tensor(q[:, cols], q[:, cols], squares[:, 2, cols], ADD)
+            for g in range(HALVES):
+                nc.vector.tensor_tensor(squares[g][:, 0, :], first_squares[g], squares[g][:, 1, :], ADD)
+            for g, cols in enumerate(halves):
+                nc.vector.tensor_tensor(q[:, cols], squares[g][:, 0, :], squares[g][:, 2, :], ADD)
             for cols in halves:
                 nc.gpsimd.tensor_tensor(k11q[:, cols], q[:, cols], k11_sb[:, cols], MULT)
+            slope = [held.tile([P, H], F32, name=f"slope{g}", tag=tags[g]) for g in range(HALVES)]
             for g, cols in enumerate(halves):
-                nc.vector.scalar_tensor_tensor(slope[:, cols], h_ps[g][:], INV_SQRT_P, k00_sb[:, cols], MULT, MULT)
-            for cols in halves:
-                nc.vector.tensor_tensor(slope[:, cols], slope[:, cols], k1_sb[:, cols], ADD)
+                nc.vector.scalar_tensor_tensor(slope[g][:], h_ps[g][:], INV_SQRT_P, k00_sb[:, cols], MULT, MULT)
             for g, cols in enumerate(halves):
-                nc.vector.scalar_tensor_tensor(slope[:, cols], h_ps[g][:], INV_SQRT_P, slope[:, cols], MULT, MULT)
+                nc.vector.tensor_tensor(slope[g][:], slope[g][:], k1_sb[:, cols], ADD)
+            for g in range(HALVES):
+                nc.vector.scalar_tensor_tensor(slope[g][:], h_ps[g][:], INV_SQRT_P, slope[g][:], MULT, MULT)
 
             pieces = [slice(j * W, (j + 1) * W) for j in range(PIECES)]
             p_ps = {}
             for step in range(PIECES + 1):
                 if step < PIECES:
                     a_bf = work.tile([P, W], BF16, name="a_bf")
-                    nc.vector.tensor_tensor(a_bf[:], slope[:, pieces[step]], k11q[:, pieces[step]], ADD)
+                    half, start = divmod(step * W, H)
+                    nc.vector.scalar_tensor_tensor(
+                        a_bf[:], k11q[:, pieces[step]], INV_SQRT_R, slope[half][:, start : start + W], MULT, ADD
+                    )
                     p_ps[step] = psum.tile([P, W], F32, name=f"p_ps{step}", tag=f"p_bank{step}")
                     nc.tensor.matmul(p_ps[step][:], wprod_sb[:], a_bf[:], start=True, stop=True)
                 if step > 0:

@@ -107,8 +107,8 @@ def tile_corrproductblock_kernel(tc, table, w, k1, k00, k11, hv, wprod, wout, of
                 nc.vector.tensor_tensor(squares[g][:, 0, :], first_squares[g], squares[g][:, 1, :], ADD)
             for g, cols in enumerate(halves):
                 nc.vector.tensor_tensor(q[:, cols], squares[g][:, 0, :], squares[g][:, 2, :], ADD)
-            for cols in halves:
-                nc.gpsimd.tensor_tensor(k11q[:, cols], q[:, cols], k11_sb[:, cols], MULT)
+            for engine, cols in zip((nc.vector, nc.gpsimd), halves):
+                engine.tensor_tensor(k11q[:, cols], q[:, cols], k11_sb[:, cols], MULT)
             slope = [held.tile([P, H], F32, name=f"slope{g}", tag=tags[g]) for g in range(HALVES)]
             for g, cols in enumerate(halves):
                 nc.vector.scalar_tensor_tensor(slope[g][:], h_ps[g][:], INV_SQRT_P, k00_sb[:, cols], MULT, MULT)

import math

import concourse.mybir as mybir
from concourse.masks import make_identity

P = 128
S = 1024
N = 512
R = 3
HALVES = 2
RUN = S // (HALVES * P)
PAIR = 2
H = N // HALVES
PIECES = 4
W = N // PIECES

FLOPS = 4 * 2 * P * P * N

BF16 = mybir.dt.bfloat16
F32 = mybir.dt.float32
U16 = mybir.dt.uint16
MULT = mybir.AluOpType.mult
ADD = mybir.AluOpType.add
COPY = mybir.ActivationFunctionType.Copy
SQUARE = mybir.ActivationFunctionType.Square

INV_SQRT_P = 1.0 / math.sqrt(P)
INV_SQRT_R = 1.0 / math.sqrt(R)


def tile_corrproductblock_kernel(tc, table, w, k1, k00, k11, hv, wprod, wout, offs, out):
    nc = tc.nc
    with tc.tile_pool(name="held", bufs=1) as held, tc.tile_pool(name="work", bufs=PIECES) as work:
        rows = [held.tile([P, RUN, P], BF16, name=f"rows{g}", tag=f"rows{g}_and_later") for g in range(HALVES)]
        table_runs = table.rearrange("(g p b) d -> p g b d", g=HALVES, p=P, b=RUN)
        for g in range(HALVES):
            nc.sync.dma_start(rows[g][:], table_runs[:, g, :, :])
        hv_sb = held.tile([P, R, N], F32, name="hv_sb")
        for c in range(R - 1):
            nc.sync.dma_start(hv_sb[:, c, :], hv[:, c, :])
        offsets = held.tile([P, N // 16], U16, name="offsets")
        nc.sync.dma_start(offsets[:], offs)
        w_sb = held.tile([P, 2 * P], BF16, name="w_sb")
        nc.sync.dma_start(w_sb[:], w)
        nc.sync.dma_start(hv_sb[:, R - 1, :], hv[:, R - 1, :])
        k11_sb = held.tile([P, N], F32, name="k11_sb")
        nc.sync.dma_start(k11_sb[:], k11)
        k00_sb = held.tile([P, N], F32, name="k00_sb")
        nc.sync.dma_start(k00_sb[:], k00)
        k1_sb = held.tile([P, N], F32, name="k1_sb")
        nc.sync.dma_start(k1_sb[:], k1)
        wprod_sb = held.tile([P, P], BF16, name="wprod_sb")
        nc.sync.dma_start(wprod_sb[:], wprod)
        wout_sb = held.tile([P, P], BF16, name="wout_sb")
        nc.sync.dma_start(wout_sb[:], wout)

        identity = held.tile([P, P], BF16, name="identity", tag="identity_and_later")
        make_identity(nc, identity[:])

        window = held.tile([P, S], BF16, name="window")
        window_runs = window[:].rearrange("d (g p b) -> d g p b", g=HALVES, p=P, b=RUN)
        with tc.psum_pool(name="early_psum", bufs=1) as early_psum:
            for g in range(HALVES):
                for first in range(0, RUN, PAIR):
                    flipped = early_psum.tile([P, PAIR, P], BF16, name=f"flipped{g}{first}")
                    for b in range(PAIR):
                        nc.tensor.transpose(flipped[:, b, :], rows[g][:, first + b, :], identity[:])
                    columns = window_runs[:, g, :, first : first + PAIR]
                    if first == 0:
                        nc.scalar.copy(columns, flipped[:].rearrange("d b p -> d p b"))
                    else:
                        nc.vector.tensor_copy(columns, flipped[:].rearrange("d b p -> d p b"))

        with tc.psum_pool(name="psum", bufs=1) as psum:
            h_ps = [psum.tile([P, H], F32, name=f"h_ps{g}", tag=f"p_bank{PIECES - HALVES + g}") for g in range(HALVES)]
            for g in range(HALVES):
                nc.tensor.matmul(
                    h_ps[g][:],
                    w_sb[:, 0:P],
                    window[:].indirect(offsets[:, g * (H // 16) : (g + 1) * (H // 16)]),
                    start=True,
                    stop=True,
                )
            out_ps = [psum.tile([P, W], F32, name=f"out_ps{j}") for j in range(PIECES)]
            for j in range(PIECES):
                nc.tensor.matmul(
                    out_ps[j][:],
                    w_sb[:, P : 2 * P],
                    window[:].indirect(offsets[:, j * (W // 16) : (j + 1) * (W // 16)]),
                    start=True,
                    stop=False,
                )

            halves = [slice(g * H, (g + 1) * H) for g in range(HALVES)]
            tags = ["rows1_and_later", "identity_and_later"]
            squares = [held.tile([P, R, H], F32, name=f"squares{g}", tag=tags[g]) for g in range(HALVES)]
            early_square = held.tile([P, H], F32, name="early_square")
            first_squares = [early_square[:], squares[1][:, 0, :]]
            for g, engine in enumerate((nc.gpsimd, nc.vector)):
                engine.tensor_tensor(first_squares[g], hv_sb[:, 0, halves[g]], hv_sb[:, 0, halves[g]], MULT)
            for c in range(1, R):
                for g, cols in enumerate(halves):
                    nc.scalar.activation(squares[g][:, c, :], hv_sb[:, c, cols], SQUARE)
            q = held.tile([P, N], F32, name="q")
            k11q = held.tile([P, N], F32, name="k11q")
            for g in range(HALVES):
                nc.vector.tensor_tensor(squares[g][:, 0, :], first_squares[g], squares[g][:, 1, :], ADD)
            for g, cols in enumerate(halves):
                nc.vector.tensor_tensor(q[:, cols], squares[g][:, 0, :], squares[g][:, 2, :], ADD)
            for engine, cols in zip((nc.vector, nc.gpsimd), halves):
                engine.tensor_tensor(k11q[:, cols], q[:, cols], k11_sb[:, cols], MULT)
            slope = [held.tile([P, H], F32, name=f"slope{g}", tag=tags[g]) for g in range(HALVES)]
            for g, cols in enumerate(halves):
                nc.vector.scalar_tensor_tensor(slope[g][:], h_ps[g][:], INV_SQRT_P, k00_sb[:, cols], MULT, MULT)
            for g, cols in enumerate(halves):
                nc.vector.tensor_tensor(slope[g][:], slope[g][:], k1_sb[:, cols], ADD)
            for g in range(HALVES):
                nc.vector.scalar_tensor_tensor(slope[g][:], h_ps[g][:], INV_SQRT_P, slope[g][:], MULT, MULT)

            pieces = [slice(j * W, (j + 1) * W) for j in range(PIECES)]
            p_ps = {}
            for step in range(PIECES + 1):
                if step < PIECES:
                    a_bf = work.tile([P, W], BF16, name="a_bf")
                    half, start = divmod(step * W, H)
                    nc.vector.scalar_tensor_tensor(
                        a_bf[:], k11q[:, pieces[step]], INV_SQRT_R, slope[half][:, start : start + W], MULT, ADD
                    )
                    p_ps[step] = psum.tile([P, W], F32, name=f"p_ps{step}", tag=f"p_bank{step}")
                    nc.tensor.matmul(p_ps[step][:], wprod_sb[:], a_bf[:], start=True, stop=True)
                if step > 0:
                    p_bf = work.tile([P, W], BF16, name="p_bf")
                    if step - 1 < PIECES // 2:
                        nc.scalar.activation(p_bf[:], p_ps[step - 1][:], COPY, scale=INV_SQRT_P)
                    else:
                        nc.vector.tensor_scalar_mul(p_bf[:], p_ps[step - 1][:], INV_SQRT_P)
                    nc.tensor.matmul(out_ps[step - 1][:], wout_sb[:], p_bf[:], start=False, stop=True)
            for j in range(PIECES):
                out_sb = work.tile([P, W], F32, name="out_sb")
                if j < PIECES // 2:
                    nc.scalar.activation(out_sb[:], out_ps[j][:], COPY, scale=INV_SQRT_P)
                else:
                    nc.vector.tensor_scalar_mul(out_sb[:], out_ps[j][:], INV_SQRT_P)
                queue = nc.scalar if j < PIECES // 2 else nc.sync
                queue.dma_start(out[:, pieces[j]], out_sb[:])
